import numpy as np
import ml_dtypes

BF16 = ml_dtypes.bfloat16


def bf(x):
    return np.asarray(x, np.float32).astype(BF16)


def f32(x):
    return np.asarray(x, np.float32)


def f64(x):
    return np.asarray(x).astype(np.float64)


def striped(idx):
    return np.tile(idx.reshape(-1, 16).T, (8, 1))


S, E, M, N = 512, 128, 128, 128
SIGMA, PSCALE = 0.25, 8.0


def setup_inputs():
    return {"table": bf(SIGMA * np.random.standard_normal((S, E))), "gold": bf(SIGMA * np.random.standard_normal((E, M))), "pred": f32(PSCALE * np.random.random((M, N))), "offs": striped(np.random.permutation(S)[:N])}


def reference(table, gold, pred, offs):
    idx = offs[:16].T.reshape(-1)
    t = f64(table)[idx].T
    u = f64(gold)
    cross = u.T @ t
    d2 = (t**2).sum(0)[None, :] + (u**2).sum(0)[:, None] - 2.0 * cross
    return np.abs(np.sqrt(d2) - f64(pred))

@@ -1,0 +1,61 @@
+import concourse.mybir as mybir
+from concourse.masks import make_identity
+
+P = 128
+S, E, M, N = 512, 128, 128, 128
+BLOCKS = S // P
+BF16, F32, U16 = mybir.dt.bfloat16, mybir.dt.float32, mybir.dt.uint16
+ALU = mybir.AluOpType
+ACT = mybir.ActivationFunctionType
+SQRT_FLOOR = 1e-30
+
+FLOPS = 2 * E * M * N
+
+
+def tile_emblosscriterion_kernel(tc, table, gold, pred, offs, out):
+    nc = tc.nc
+    with (
+        tc.tile_pool(name="held", bufs=1) as held,
+        tc.psum_pool(name="psum", bufs=1) as psum,
+    ):
+        offsets = held.tile([P, N // 16], U16, name="offsets")
+        nc.sync.dma_start(offsets[:], offs)
+        words = held.tile([P, BLOCKS, E], BF16, name="words")
+        nc.sync.dma_start(words[:], table.rearrange("(b p) e -> p b e", p=P))
+        gold_sb = held.tile([E, M], BF16, name="gold_sb")
+        nc.scalar.dma_start(gold_sb[:], gold)
+        pred_sb = held.tile([M, N], F32, name="pred_sb")
+        nc.scalar.dma_start(pred_sb[:], pred)
+
+        identity = held.tile([P, P], BF16, name="identity")
+        make_identity(nc, identity[:])
+        minus_half = held.tile([P, P], BF16, name="minus_half")
+        nc.vector.memset(minus_half[:], -0.5)
+
+        flipped = psum.tile([E, S], BF16, name="flipped")
+        for b in range(BLOCKS):
+            nc.tensor.transpose(flipped[:, b * P : (b + 1) * P], words[:, b, :], identity[:])
+        table_t = held.tile([E, S], BF16, name="table_t")
+        nc.vector.tensor_copy(table_t[:], flipped[:])
+
+        picked = psum.tile([E, N], F32, name="picked")
+        nc.tensor.matmul(picked[:], identity[:], table_t[:].indirect(offsets[:]), start=True, stop=True)
+        picked_sq = held.tile([E, N], BF16, name="picked_sq")
+        nc.scalar.activation(picked_sq[:], picked[:], ACT.Square)
+        gold_sq = held.tile([E, M], BF16, name="gold_sq")
+        nc.vector.tensor_tensor(gold_sq[:], gold_sb[:], gold_sb[:], ALU.mult)
+
+        acc = psum.tile([M, N], F32, name="acc")
+        nc.tensor.matmul(acc[:], gold_sb[:], table_t[:].indirect(offsets[:]), start=True, stop=False)
+        nc.tensor.matmul(acc[:], gold_sq[:], minus_half[:], start=False, stop=False)
+        nc.tensor.matmul(acc[:], minus_half[:], picked_sq[:], start=False, stop=True)
+
+        d2 = held.tile([M, N], F32, name="d2")
+        nc.vector.tensor_scalar(d2[:], acc[:], -2.0, SQRT_FLOOR, ALU.mult, ALU.max)
+        dist = held.tile([M, N], F32, name="dist")
+        nc.scalar.activation(dist[:], d2[:], ACT.Sqrt)
+        diff = held.tile([M, N], F32, name="diff")
+        nc.vector.tensor_tensor(diff[:], dist[:], pred_sb[:], ALU.subtract)
+        loss = held.tile([M, N], F32, name="loss")
+        nc.vector.scalar_tensor_tensor(loss[:], diff[:], -1.0, diff[:], ALU.mult, ALU.max)
+        nc.sync.dma_start(out, loss[:])

@@ -32,6 +32,11 @@ def tile_emblosscriterion_kernel(tc, table, gold, pred, offs, out):
         minus_half = held.tile([P, P], BF16, name="minus_half")
         nc.vector.memset(minus_half[:], -0.5)
 
+        scratch = held.tile([P, 1], F32, name="scratch")
+        nc.vector.memset(scratch[:], 1.0)
+        scratch_root = held.tile([P, 1], F32, name="scratch_root")
+        nc.scalar.activation(scratch_root[:], scratch[:], ACT.Sqrt)
+
         flipped = psum.tile([E, S], BF16, name="flipped")
         for b in range(BLOCKS):
             nc.tensor.transpose(flipped[:, b * P : (b + 1) * P], words[:, b, :], identity[:])

@@ -18,12 +18,14 @@ def tile_emblosscriterion_kernel(tc, table, gold, pred, offs, out):
         tc.tile_pool(name="held", bufs=1) as held,
         tc.psum_pool(name="psum", bufs=1) as psum,
     ):
+        words = [held.tile([P, E], BF16, name=f"words{b}") for b in range(BLOCKS)]
+        for b in range(BLOCKS):
+            queue = nc.sync if b % 2 == 0 else nc.scalar
+            queue.dma_start(words[b][:], table[b * P : (b + 1) * P, :])
         offsets = held.tile([P, N // 16], U16, name="offsets")
         nc.sync.dma_start(offsets[:], offs)
-        words = held.tile([P, BLOCKS, E], BF16, name="words")
-        nc.sync.dma_start(words[:], table.rearrange("(b p) e -> p b e", p=P))
         gold_sb = held.tile([E, M], BF16, name="gold_sb")
-        nc.scalar.dma_start(gold_sb[:], gold)
+        nc.sync.dma_start(gold_sb[:], gold)
         pred_sb = held.tile([M, N], F32, name="pred_sb")
         nc.scalar.dma_start(pred_sb[:], pred)
 
@@ -37,11 +39,14 @@ def tile_emblosscriterion_kernel(tc, table, gold, pred, offs, out):
         scratch_root = held.tile([P, 1], F32, name="scratch_root")
         nc.scalar.activation(scratch_root[:], scratch[:], ACT.Sqrt)
 
-        flipped = psum.tile([E, S], BF16, name="flipped")
-        for b in range(BLOCKS):
-            nc.tensor.transpose(flipped[:, b * P : (b + 1) * P], words[:, b, :], identity[:])
         table_t = held.tile([E, S], BF16, name="table_t")
-        nc.vector.tensor_copy(table_t[:], flipped[:])
+        for b in range(BLOCKS):
+            flipped = psum.tile([E, P], BF16, name=f"flipped{b}")
+            nc.tensor.transpose(flipped[:], words[b][:], identity[:])
+            if b % 2 == 0:
+                nc.vector.tensor_copy(table_t[:, b * P : (b + 1) * P], flipped[:])
+            else:
+                nc.scalar.copy(table_t[:, b * P : (b + 1) * P], flipped[:])
 
         picked = psum.tile([E, N], F32, name="picked")
         nc.tensor.matmul(picked[:], identity[:], table_t[:].indirect(offsets[:]), start=True, stop=True)

@@ -60,12 +60,17 @@ def tile_emblosscriterion_kernel(tc, table, gold, pred, offs, out):
         nc.tensor.matmul(acc[:], gold_sq[:], minus_half[:], start=False, stop=False)
         nc.tensor.matmul(acc[:], minus_half[:], picked_sq[:], start=False, stop=True)
 
+        halves = [slice(h * (N // 2), (h + 1) * (N // 2)) for h in range(2)]
         d2 = held.tile([M, N], F32, name="d2")
-        nc.vector.tensor_scalar(d2[:], acc[:], -2.0, SQRT_FLOOR, ALU.mult, ALU.max)
+        for cols in halves:
+            nc.vector.tensor_scalar(d2[:, cols], acc[:, cols], -2.0, SQRT_FLOOR, ALU.mult, ALU.max)
         dist = held.tile([M, N], F32, name="dist")
-        nc.scalar.activation(dist[:], d2[:], ACT.Sqrt)
+        for cols in halves:
+            nc.scalar.activation(dist[:, cols], d2[:, cols], ACT.Sqrt)
         diff = held.tile([M, N], F32, name="diff")
-        nc.vector.tensor_tensor(diff[:], dist[:], pred_sb[:], ALU.subtract)
+        for cols in halves:
+            nc.vector.tensor_tensor(diff[:, cols], dist[:, cols], pred_sb[:, cols], ALU.subtract)
         loss = held.tile([M, N], F32, name="loss")
-        nc.vector.scalar_tensor_tensor(loss[:], diff[:], -1.0, diff[:], ALU.mult, ALU.max)
+        for cols in halves:
+            nc.vector.scalar_tensor_tensor(loss[:, cols], diff[:, cols], -1.0, diff[:, cols], ALU.mult, ALU.max)
         nc.sync.dma_start(out, loss[:])

@@ -27,7 +27,7 @@ def tile_emblosscriterion_kernel(tc, table, gold, pred, offs, out):
         gold_sb = held.tile([E, M], BF16, name="gold_sb")
         nc.sync.dma_start(gold_sb[:], gold)
         pred_sb = held.tile([M, N], F32, name="pred_sb")
-        nc.scalar.dma_start(pred_sb[:], pred)
+        nc.sync.dma_start(pred_sb[:], pred)
 
         identity = held.tile([P, P], BF16, name="identity")
         make_identity(nc, identity[:])
@@ -43,10 +43,7 @@ def tile_emblosscriterion_kernel(tc, table, gold, pred, offs, out):
         for b in range(BLOCKS):
             flipped = psum.tile([E, P], BF16, name=f"flipped{b}")
             nc.tensor.transpose(flipped[:], words[b][:], identity[:])
-            if b % 2 == 0:
-                nc.vector.tensor_copy(table_t[:, b * P : (b + 1) * P], flipped[:])
-            else:
-                nc.scalar.copy(table_t[:, b * P : (b + 1) * P], flipped[:])
+            nc.vector.tensor_copy(table_t[:, b * P : (b + 1) * P], flipped[:])
 
         picked = psum.tile([E, N], F32, name="picked")
         nc.tensor.matmul(picked[:], identity[:], table_t[:].indirect(offsets[:]), start=True, stop=True)

@@ -57,7 +57,7 @@ def tile_emblosscriterion_kernel(tc, table, gold, pred, offs, out):
         nc.tensor.matmul(acc[:], gold_sq[:], minus_half[:], start=False, stop=False)
         nc.tensor.matmul(acc[:], minus_half[:], picked_sq[:], start=False, stop=True)
 
-        halves = [slice(h * (N // 2), (h + 1) * (N // 2)) for h in range(2)]
+        halves = [slice(h * (N // 4), (h + 1) * (N // 4)) for h in range(4)]
         d2 = held.tile([M, N], F32, name="d2")
         for cols in halves:
             nc.vector.tensor_scalar(d2[:, cols], acc[:, cols], -2.0, SQRT_FLOOR, ALU.mult, ALU.max)

@@ -50,24 +50,24 @@ def tile_emblosscriterion_kernel(tc, table, gold, pred, offs, out):
         picked_sq = held.tile([E, N], BF16, name="picked_sq")
         nc.scalar.activation(picked_sq[:], picked[:], ACT.Square)
         gold_sq = held.tile([E, M], BF16, name="gold_sq")
-        nc.vector.tensor_tensor(gold_sq[:], gold_sb[:], gold_sb[:], ALU.mult)
+        nc.scalar.activation(gold_sq[:], gold_sb[:], ACT.Square)
 
         acc = psum.tile([M, N], F32, name="acc")
         nc.tensor.matmul(acc[:], gold_sb[:], table_t[:].indirect(offsets[:]), start=True, stop=False)
         nc.tensor.matmul(acc[:], gold_sq[:], minus_half[:], start=False, stop=False)
         nc.tensor.matmul(acc[:], minus_half[:], picked_sq[:], start=False, stop=True)
 
-        halves = [slice(h * (N // 4), (h + 1) * (N // 4)) for h in range(4)]
+        quarters = [slice(h * (N // 4), (h + 1) * (N // 4)) for h in range(4)]
         d2 = held.tile([M, N], F32, name="d2")
-        for cols in halves:
+        for cols in quarters:
             nc.vector.tensor_scalar(d2[:, cols], acc[:, cols], -2.0, SQRT_FLOOR, ALU.mult, ALU.max)
         dist = held.tile([M, N], F32, name="dist")
-        for cols in halves:
+        for cols in quarters:
             nc.scalar.activation(dist[:, cols], d2[:, cols], ACT.Sqrt)
         diff = held.tile([M, N], F32, name="diff")
-        for cols in halves:
+        for cols in quarters:
             nc.vector.tensor_tensor(diff[:, cols], dist[:, cols], pred_sb[:, cols], ALU.subtract)
         loss = held.tile([M, N], F32, name="loss")
-        for cols in halves:
+        for cols in quarters:
             nc.vector.scalar_tensor_tensor(loss[:, cols], diff[:, cols], -1.0, diff[:, cols], ALU.mult, ALU.max)
         nc.sync.dma_start(out, loss[:])

@@ -52,18 +52,20 @@ def tile_emblosscriterion_kernel(tc, table, gold, pred, offs, out):
         gold_sq = held.tile([E, M], BF16, name="gold_sq")
         nc.scalar.activation(gold_sq[:], gold_sb[:], ACT.Square)
 
+        gold_norm = psum.tile([M, 1], F32, name="gold_norm", tag="flipped2")
+        nc.tensor.matmul(gold_norm[:], gold_sq[:], minus_half[:, 0:1], start=True, stop=True)
+
         acc = psum.tile([M, N], F32, name="acc")
         nc.tensor.matmul(acc[:], gold_sb[:], table_t[:].indirect(offsets[:]), start=True, stop=False)
-        nc.tensor.matmul(acc[:], gold_sq[:], minus_half[:], start=False, stop=False)
         nc.tensor.matmul(acc[:], minus_half[:], picked_sq[:], start=False, stop=True)
 
         quarters = [slice(h * (N // 4), (h + 1) * (N // 4)) for h in range(4)]
-        d2 = held.tile([M, N], F32, name="d2")
+        minus_half_d2 = held.tile([M, N], F32, name="minus_half_d2")
         for cols in quarters:
-            nc.vector.tensor_scalar(d2[:, cols], acc[:, cols], -2.0, SQRT_FLOOR, ALU.mult, ALU.max)
+            nc.vector.tensor_scalar(minus_half_d2[:, cols], acc[:, cols], gold_norm[:], -0.5 * SQRT_FLOOR, ALU.add, ALU.min)
         dist = held.tile([M, N], F32, name="dist")
         for cols in quarters:
-            nc.scalar.activation(dist[:, cols], d2[:, cols], ACT.Sqrt)
+            nc.scalar.activation(dist[:, cols], minus_half_d2[:, cols], ACT.Sqrt, scale=-2.0)
         diff = held.tile([M, N], F32, name="diff")
         for cols in quarters:
             nc.vector.tensor_tensor(diff[:, cols], dist[:, cols], pred_sb[:, cols], ALU.subtract)

@@ -47,22 +47,29 @@ def tile_emblosscriterion_kernel(tc, table, gold, pred, offs, out):
 
         picked = psum.tile([E, N], F32, name="picked")
         nc.tensor.matmul(picked[:], identity[:], table_t[:].indirect(offsets[:]), start=True, stop=True)
-        picked_sq = held.tile([E, N], BF16, name="picked_sq")
-        nc.scalar.activation(picked_sq[:], picked[:], ACT.Square)
+        HALF = N // 2
+        picked_sq = [held.tile([E, HALF], BF16, name=f"picked_sq{h}") for h in range(2)]
+        for h in range(2):
+            nc.scalar.activation(picked_sq[h][:], picked[:, h * HALF : (h + 1) * HALF], ACT.Square)
         gold_sq = held.tile([E, M], BF16, name="gold_sq")
         nc.scalar.activation(gold_sq[:], gold_sb[:], ACT.Square)
 
         gold_norm = psum.tile([M, 1], F32, name="gold_norm", tag="flipped2")
         nc.tensor.matmul(gold_norm[:], gold_sq[:], minus_half[:, 0:1], start=True, stop=True)
 
-        acc = psum.tile([M, N], F32, name="acc")
-        nc.tensor.matmul(acc[:], gold_sb[:], table_t[:].indirect(offsets[:]), start=True, stop=False)
-        nc.tensor.matmul(acc[:], minus_half[:], picked_sq[:], start=False, stop=True)
+        acc = [psum.tile([M, HALF], F32, name=f"acc{h}") for h in range(2)]
+        half_columns = HALF // 16
+        for h in range(2):
+            part = offsets[:, h * half_columns : (h + 1) * half_columns]
+            nc.tensor.matmul(acc[h][:], gold_sb[:], table_t[:].indirect(part), start=True, stop=False)
+        for h in range(2):
+            nc.tensor.matmul(acc[h][:], minus_half[:], picked_sq[h][:], start=False, stop=True)
 
         quarters = [slice(h * (N // 4), (h + 1) * (N // 4)) for h in range(4)]
         minus_half_d2 = held.tile([M, N], F32, name="minus_half_d2")
-        for cols in quarters:
-            nc.vector.tensor_scalar(minus_half_d2[:, cols], acc[:, cols], gold_norm[:], -0.5 * SQRT_FLOOR, ALU.add, ALU.min)
+        for q, cols in enumerate(quarters):
+            within_half = slice(q % 2 * (N // 4), (q % 2 + 1) * (N // 4))
+            nc.vector.tensor_scalar(minus_half_d2[:, cols], acc[q // 2][:, within_half], gold_norm[:], -0.5 * SQRT_FLOOR, ALU.add, ALU.min)
         dist = held.tile([M, N], F32, name="dist")
         for cols in quarters:
             nc.scalar.activation(dist[:, cols], minus_half_d2[:, cols], ACT.Sqrt, scale=-2.0)

@@ -22,10 +22,10 @@ def tile_emblosscriterion_kernel(tc, table, gold, pred, offs, out):
         for b in range(BLOCKS):
             queue = nc.sync if b % 2 == 0 else nc.scalar
             queue.dma_start(words[b][:], table[b * P : (b + 1) * P, :])
-        offsets = held.tile([P, N // 16], U16, name="offsets")
-        nc.sync.dma_start(offsets[:], offs)
         gold_sb = held.tile([E, M], BF16, name="gold_sb")
         nc.sync.dma_start(gold_sb[:], gold)
+        offsets = held.tile([P, N // 16], U16, name="offsets")
+        nc.sync.dma_start(offsets[:], offs)
         pred_sb = held.tile([M, N], F32, name="pred_sb")
         nc.sync.dma_start(pred_sb[:], pred)
 

import concourse.mybir as mybir
from concourse.masks import make_identity

P = 128
S, E, M, N = 512, 128, 128, 128
BLOCKS = S // P
BF16, F32, U16 = mybir.dt.bfloat16, mybir.dt.float32, mybir.dt.uint16
ALU = mybir.AluOpType
ACT = mybir.ActivationFunctionType
SQRT_FLOOR = 1e-30

FLOPS = 2 * E * M * N


def tile_emblosscriterion_kernel(tc, table, gold, pred, offs, out):
    nc = tc.nc
    with (
        tc.tile_pool(name="held", bufs=1) as held,
        tc.psum_pool(name="psum", bufs=1) as psum,
    ):
        words = [held.tile([P, E], BF16, name=f"words{b}") for b in range(BLOCKS)]
        for b in range(BLOCKS):
            queue = nc.sync if b % 2 == 0 else nc.scalar
            queue.dma_start(words[b][:], table[b * P : (b + 1) * P, :])
        gold_sb = held.tile([E, M], BF16, name="gold_sb")
        nc.sync.dma_start(gold_sb[:], gold)
        offsets = held.tile([P, N // 16], U16, name="offsets")
        nc.sync.dma_start(offsets[:], offs)
        pred_sb = held.tile([M, N], F32, name="pred_sb")
        nc.sync.dma_start(pred_sb[:], pred)

        identity = held.tile([P, P], BF16, name="identity")
        make_identity(nc, identity[:])
        minus_half = held.tile([P, P], BF16, name="minus_half")
        nc.vector.memset(minus_half[:], -0.5)

        scratch = held.tile([P, 1], F32, name="scratch")
        nc.vector.memset(scratch[:], 1.0)
        scratch_root = held.tile([P, 1], F32, name="scratch_root")
        nc.scalar.activation(scratch_root[:], scratch[:], ACT.Sqrt)

        table_t = held.tile([E, S], BF16, name="table_t")
        for b in range(BLOCKS):
            flipped = psum.tile([E, P], BF16, name=f"flipped{b}")
            nc.tensor.transpose(flipped[:], words[b][:], identity[:])
            nc.vector.tensor_copy(table_t[:, b * P : (b + 1) * P], flipped[:])

        picked = psum.tile([E, N], F32, name="picked")
        nc.tensor.matmul(picked[:], identity[:], table_t[:].indirect(offsets[:]), start=True, stop=True)
        HALF = N // 2
        picked_sq = [held.tile([E, HALF], BF16, name=f"picked_sq{h}") for h in range(2)]
        for h in range(2):
            nc.scalar.activation(picked_sq[h][:], picked[:, h * HALF : (h + 1) * HALF], ACT.Square)
        gold_sq = held.tile([E, M], BF16, name="gold_sq")
        nc.scalar.activation(gold_sq[:], gold_sb[:], ACT.Square)

        gold_norm = psum.tile([M, 1], F32, name="gold_norm", tag="flipped2")
        nc.tensor.matmul(gold_norm[:], gold_sq[:], minus_half[:, 0:1], start=True, stop=True)

        acc = [psum.tile([M, HALF], F32, name=f"acc{h}") for h in range(2)]
        half_columns = HALF // 16
        for h in range(2):
            part = offsets[:, h * half_columns : (h + 1) * half_columns]
            nc.tensor.matmul(acc[h][:], gold_sb[:], table_t[:].indirect(part), start=True, stop=False)
        for h in range(2):
            nc.tensor.matmul(acc[h][:], minus_half[:], picked_sq[h][:], start=False, stop=True)

        quarters = [slice(h * (N // 4), (h + 1) * (N // 4)) for h in range(4)]
        minus_half_d2 = held.tile([M, N], F32, name="minus_half_d2")
        for q, cols in enumerate(quarters):
            within_half = slice(q % 2 * (N // 4), (q % 2 + 1) * (N // 4))
            nc.vector.tensor_scalar(minus_half_d2[:, cols], acc[q // 2][:, within_half], gold_norm[:], -0.5 * SQRT_FLOOR, ALU.add, ALU.min)
        dist = held.tile([M, N], F32, name="dist")
        for cols in quarters:
            nc.scalar.activation(dist[:, cols], minus_half_d2[:, cols], ACT.Sqrt, scale=-2.0)
        diff = held.tile([M, N], F32, name="diff")
        for cols in quarters:
            nc.vector.tensor_tensor(diff[:, cols], dist[:, cols], pred_sb[:, cols], ALU.subtract)
        loss = held.tile([M, N], F32, name="loss")
        for cols in quarters:
            nc.vector.scalar_tensor_tensor(loss[:, cols], diff[:, cols], -1.0, diff[:, cols], ALU.mult, ALU.max)
        nc.sync.dma_start(out, loss[:])
